import numpy as np
import ml_dtypes


def mxq(x, axis, fmt="e4m3"):
    dtype, down = {"e4m3": (ml_dtypes.float8_e4m3fn, 7), "e5m2": (ml_dtypes.float8_e5m2, 14)}[fmt]
    v = np.moveaxis(np.asarray(x, np.float32).astype(ml_dtypes.bfloat16).astype(np.float64), axis, -1)
    blocks = v.reshape(v.shape[:-1] + (-1, 32))
    amax = np.abs(blocks).max(-1, keepdims=True)
    byte = np.maximum(np.where(amax > 0, np.frexp(amax)[1] - 1 + 127, 0) - down, 1)
    scale = np.exp2(byte - 127.0)
    codes = (blocks / scale).astype(np.float32).astype(dtype).astype(np.float64)
    return np.moveaxis((codes * scale).reshape(v.shape), -1, axis)


WIDE = False


def mx_kscale(k):
    if not WIDE:
        return np.ones(k)
    levels = np.array([10, -10, 5, -5, 0])
    a = np.random.permutation(np.resize(levels, k // 512 * 4)).reshape(k // 512, 4)
    idx = np.arange(k)
    return np.exp2(a[idx // 512, idx % 128 // 32])


BF16 = ml_dtypes.bfloat16


def bf(x):
    return np.asarray(x, np.float32).astype(BF16)


def f64(x):
    return np.asarray(x).astype(np.float64)


E2M1 = np.array([0.0, 0.5, 1.0, 1.5, 2.0, 3.0, 4.0, 6.0, -0.0, -0.5, -1.0, -1.5, -2.0, -3.0, -4.0, -6.0])


def pack_weight(w, fmt):
    k, n = w.shape
    w = f64(bf(w)).reshape(k // 32, 32, n)
    amax = np.abs(w).max(1)
    if fmt == "e4m3":
        byte = np.frexp(amax)[1] - 1 + 127 - 7
    else:
        mant, ex = np.frexp(amax / 6.0)
        byte = np.where(mant > 0.5, ex, ex - 1) + 127
    byte = np.clip(np.where(amax > 0, byte, 1), 1, 254)
    scaled = (w * np.exp2(127.0 - byte)[:, None, :]).reshape(k, n).astype(np.float32)
    by_word = np.ascontiguousarray(scaled.reshape(k // 512, 128, 4, n).transpose(0, 1, 3, 2))
    if fmt == "e4m3":
        words = by_word.astype(ml_dtypes.float8_e4m3fn).view(np.uint8)
    else:
        c = by_word.astype(ml_dtypes.float4_e2m1fn).view(np.uint8) & 0xF
        words = c[..., 0::2] | (c[..., 1::2] << 4)
    return np.ascontiguousarray(words), np.ascontiguousarray(byte.astype(np.uint8).reshape(k // 512, 16, n))


def unpack_weight(words, scales, fmt):
    g, p, n, _ = words.shape
    if fmt == "e4m3":
        vals = np.ascontiguousarray(words).view(ml_dtypes.float8_e4m3fn).astype(np.float64)
    else:
        nib = np.empty((g, p, n, 4), np.uint8)
        nib[..., 0::2] = words & 0xF
        nib[..., 1::2] = words >> 4
        vals = E2M1[nib]
    vals = vals * np.repeat(np.exp2(scales.astype(np.float64) - 127.0), 8, axis=1)[..., None]
    return vals.transpose(0, 1, 3, 2).reshape(g * 512, n)

def pack4(w):
    words, scales = pack_weight(w, "e2m1")
    return words.reshape(words.shape[0], 128, -1), scales


def unpack4(words, scales):
    return unpack_weight(words.reshape(words.shape[0], 128, -1, 2), scales, "e2m1")


B, S, D, NH, NKV, HD = 1, 512, 2048, 16, 4, 128
ROPE_THETA = 10000.0


def rope_tables():
    freqs = 1.0 / (ROPE_THETA ** (f64(np.arange(0, HD, 2)) / HD))
    ang = np.outer(f64(np.arange(S)), freqs)
    return np.cos(ang), np.sin(ang)


def rope(x, cos, sin):
    xr = x.reshape(*x.shape[:-1], HD // 2, 2)
    re, im = xr[..., 0], xr[..., 1]
    c = cos[None, :, None, :]
    s = sin[None, :, None, :]
    return np.stack((re * c - im * s, re * s + im * c), axis=-1).reshape(x.shape)


def setup_inputs():
    s = mx_kscale(D)
    hidden_states = bf(np.random.standard_normal((B, S, D)) * s)
    wq_words, wq_scales = pack4(np.random.standard_normal((D, NH * HD)) / np.sqrt(D) / s[:, None])
    wk_words, wk_scales = pack4(np.random.standard_normal((D, NKV * HD)) / np.sqrt(D) / s[:, None])
    wv_words, wv_scales = pack4(np.random.standard_normal((D, NKV * HD)) * 2.0 / np.sqrt(D) / s[:, None])
    return {"hidden_states": hidden_states,
            "wq_words": wq_words, "wq_scales": wq_scales,
            "wk_words": wk_words, "wk_scales": wk_scales,
            "wv_words": wv_words, "wv_scales": wv_scales}


def reference(hidden_states, wq_words, wq_scales, wk_words, wk_scales, wv_words, wv_scales):
    xq = mxq(f64(hidden_states), 2, "e4m3")
    q = (xq @ unpack4(wq_words, wq_scales)).reshape(B, S, NH, HD)
    k = (xq @ unpack4(wk_words, wk_scales)).reshape(B, S, NKV, HD)
    v = (xq @ unpack4(wv_words, wv_scales)).reshape(B, S, NKV, HD)
    cos, sin = rope_tables()
    return rope(q, cos, sin), rope(k, cos, sin), v

@@ -1,0 +1,213 @@
+import math
+from contextlib import ExitStack
+
+import concourse.masks as masks
+import concourse.mybir as mybir
+
+F32 = mybir.dt.float32
+BF16 = mybir.dt.bfloat16
+I32 = mybir.dt.int32
+U32 = mybir.dt.uint32
+U8 = mybir.dt.uint8
+FP8X4 = mybir.dt.float8_e4m3fn_x4
+FP4X4 = mybir.dt.float4_e2m1fn_x4
+ALU = mybir.AluOpType
+ACT = mybir.ActivationFunctionType
+
+P = 128
+S = 512
+D = 2048
+HD = 128
+PAIRS = HD // 2
+K_PASS = 4 * P
+PASSES = D // K_PASS
+TOK_TILES = S // P
+BANK = 512
+HEADS_PER_BANK = BANK // HD
+ROPE_THETA = 10000.0
+FREQ_RATIO = ROPE_THETA ** (-1.0 / PAIRS)
+ROUND_MAGIC = 12582912.0
+
+FLOPS = 2 * S * D * (2048 + 512 + 512)
+
+
+def load_scale_rows(nc, plane, scales_dram, col0, width):
+    rows = scales_dram.bitcast(I32)
+    for b in range(2):
+        for r in range(4):
+            nc.sync.dma_start(
+                out=plane[32 * b + r : P : 64, :, :].bitcast(I32),
+                in_=rows[:, 4 * b + r : 16 : 8, col0 // 4 : (col0 + width) // 4].rearrange("g q n -> q g n"),
+            )
+
+
+def tile_rptattention_pa_kernel(
+    tc, hidden_states, wq_words, wq_scales, wk_words, wk_scales, wv_words, wv_scales, out_0, out_1, out_2
+):
+    nc = tc.nc
+    x_dram = hidden_states[0].rearrange("(t p) k -> t p k", p=P)
+    q_dram = out_0[0].rearrange("(t p) h d -> t p (h d)", p=P)
+    k_dram = out_1[0].rearrange("(t p) h d -> t p (h d)", p=P)
+    v_dram = out_2[0].rearrange("(t p) h d -> t p (h d)", p=P)
+
+    groups = [
+        ("k", wk_words, wk_scales, 0, BANK, k_dram, True),
+        ("q_lo", wq_words, wq_scales, 0, 2 * BANK, q_dram, True),
+        ("q_hi", wq_words, wq_scales, 2 * BANK, 2 * BANK, q_dram, True),
+        ("v", wv_words, wv_scales, 0, BANK, v_dram, False),
+    ]
+
+    with ExitStack() as ctx:
+        keep = ctx.enter_context(tc.tile_pool(name="keep", bufs=1))
+        stage = ctx.enter_context(tc.tile_pool(name="stage", bufs=4))
+        psum_t = ctx.enter_context(tc.psum_pool(name="psum_t", bufs=2))
+        psum_acc = ctx.enter_context(tc.psum_pool(name="psum_acc", bufs=6))
+
+        x_sb = []
+        for t in range(TOK_TILES):
+            x_tile = keep.tile([P, D], BF16, name="x_%d" % t)
+            nc.scalar.dma_start(out=x_tile[:], in_=x_dram[t])
+            x_sb.append(x_tile)
+
+        w_planes = {}
+        w_words = {}
+        for name, words, scales, col0, width, out_dram, rotated in groups:
+            plane = keep.tile([P, PASSES, width], U8, align_bytes=64, name="plane_%s" % name)
+            nc.vector.memset(plane[:].rearrange("p g n -> p (g n)").bitcast(I32), 0)
+            w_planes[name] = plane
+        for name, words, scales, col0, width, out_dram, rotated in groups:
+            load_scale_rows(nc, w_planes[name], scales, col0, width)
+            words_i32 = words.bitcast(I32)
+            for g in range(PASSES):
+                w_tile = keep.tile([P, 2 * width], U8, align_bytes=64, name="w_%s_%d" % (name, g))
+                nc.sync.dma_start(
+                    out=w_tile[:].bitcast(I32),
+                    in_=words_i32[g, :, col0 // 2 : (col0 + width) // 2],
+                )
+                w_words[(name, g)] = w_tile
+
+        zero = keep.tile([P, 1], F32, name="zero")
+        nc.vector.memset(zero[:], 0.0)
+        warm = keep.tile([P, 1], F32, name="warm")
+        nc.scalar.activation(out=warm[:], in_=zero[:], func=ACT.Sin)
+
+        ident = keep.tile([P, P], F32, name="ident")
+        masks.make_identity(nc, ident[:])
+
+        pos_i = keep.tile([P, TOK_TILES], I32, name="pos_i")
+        nc.gpsimd.iota(pos_i[:], pattern=[[P, TOK_TILES]], base=0, channel_multiplier=1)
+        pos = keep.tile([P, TOK_TILES], F32, name="pos")
+        nc.vector.tensor_copy(out=pos[:], in_=pos_i[:])
+
+        turns = keep.tile([P, PAIRS, 4], F32, name="turns")
+        nc.vector.memset(turns[:, 0:1, :], 1.0)
+        nc.vector.tensor_scalar(
+            out=turns[:, 0:1, :], in0=turns[:, 0:1, :], scalar1=1.0 / (2.0 * math.pi), scalar2=None, op0=ALU.mult
+        )
+        for step in range(6):
+            have = 2**step
+            nc.vector.tensor_scalar(
+                out=turns[:, have : 2 * have, :],
+                in0=turns[:, 0:have, :],
+                scalar1=FREQ_RATIO**have,
+                scalar2=None,
+                op0=ALU.mult,
+            )
+        phase = keep.tile([P, PAIRS, 2, 2], F32, name="phase")
+        nc.vector.memset(phase[:], 0.25)
+        nc.vector.memset(phase[:, :, 0, 1], 0.0)
+        nc.vector.memset(phase[:, :, 1, 0], 0.5)
+
+        rot = []
+        for t in range(TOK_TILES):
+            angle = stage.tile([P, 4 * PAIRS], F32, name="angle")
+            nc.vector.scalar_tensor_tensor(
+                out=angle[:],
+                in0=turns[:].rearrange("p j c -> p (j c)"),
+                scalar=pos[:, t : t + 1],
+                in1=phase[:].rearrange("p j i o -> p (j i o)"),
+                op0=ALU.mult,
+                op1=ALU.add,
+            )
+            shifted = stage.tile([P, 4 * PAIRS], F32, name="shifted")
+            nc.vector.tensor_scalar(out=shifted[:], in0=angle[:], scalar1=ROUND_MAGIC, scalar2=None, op0=ALU.add)
+            neg_frac = stage.tile([P, 4 * PAIRS], F32, name="neg_frac")
+            nc.vector.scalar_tensor_tensor(
+                out=neg_frac[:],
+                in0=shifted[:],
+                scalar=ROUND_MAGIC,
+                in1=angle[:],
+                op0=ALU.subtract,
+                op1=ALU.subtract,
+            )
+            rot_t = keep.tile([P, 4 * PAIRS], F32, name="rot_%d" % t)
+            nc.scalar.activation(out=rot_t[:], in_=neg_frac[:], func=ACT.Sin, scale=-2.0 * math.pi)
+            rot.append(rot_t)
+
+        x_codes = {}
+        x_scales = {}
+        for t in range(TOK_TILES):
+            x_words = x_sb[t][:].bitcast(F32)
+            for half in range(2):
+                xt = psum_t.tile([P, 2, 2, P], F32, name="xt")
+                for gg in range(2):
+                    g = 2 * half + gg
+                    for u in range(2):
+                        nc.tensor.transpose(
+                            xt[:, gg, u, :], x_words[:, 256 * g + u : 256 * (g + 1) : 2], ident[:]
+                        )
+                grouped = stage.tile([P, 2 * P * 4], BF16, align_bytes=64, name="grouped")
+                nc.scalar.copy(
+                    out=grouped[:].bitcast(F32).rearrange("p (g r u) -> p g r u", g=2, u=2),
+                    in_=xt[:].rearrange("p g u r -> p g r u"),
+                )
+                codes = keep.tile([P, 2 * P], U32, align_bytes=64, name="x_codes_%d_%d" % (t, half))
+                scales = keep.tile([P, 2 * P], U8, align_bytes=64, name="x_scales_%d_%d" % (t, half))
+                nc.vector.quantize_mx(out=codes[:].bitcast(FP8X4), scales=scales[:], in_=grouped[:])
+                for gg in range(2):
+                    x_codes[(t, 2 * half + gg)] = codes[:, gg * P : (gg + 1) * P]
+                    x_scales[(t, 2 * half + gg)] = scales[:, gg * P : (gg + 1) * P]
+
+        for name, words, scales, col0, width, out_dram, rotated in groups:
+            banks = width // BANK
+            for t in range(TOK_TILES):
+                accs = []
+                for b in range(banks):
+                    acc = psum_acc.tile([P, BANK], F32, name="acc")
+                    accs.append(acc)
+                for g in range(PASSES):
+                    for b in range(banks):
+                        nc.tensor.matmul_mx(
+                            out=accs[b][:],
+                            lhsT=x_codes[(t, g)].bitcast(FP8X4),
+                            lhsT_scale=x_scales[(t, g)],
+                            rhs=w_words[(name, g)][:, 2 * BANK * b : 2 * BANK * (b + 1)].bitcast(FP4X4),
+                            rhs_scale=w_planes[name][:, g, BANK * b : BANK * (b + 1)],
+                            start=(g == 0),
+                            stop=(g == PASSES - 1),
+                        )
+                res = keep.tile([P, width], F32, name="res_%s_%d" % (name, t))
+                for b in range(banks):
+                    res_cols = res[:, BANK * b : BANK * (b + 1)]
+                    if rotated:
+                        prod = stage.tile([P, 2 * BANK], F32, name="prod")
+                        full = [P, HEADS_PER_BANK, PAIRS, 2, 2]
+                        nc.vector.tensor_tensor(
+                            out=prod[:].rearrange("p (h j i o) -> p h j i o", h=HEADS_PER_BANK, i=2, o=2),
+                            in0=accs[b][:]
+                            .rearrange("p (h j i) -> p h j i", h=HEADS_PER_BANK, i=2)
+                            .unsqueeze(4)
+                            .to_broadcast(full),
+                            in1=rot[t][:].rearrange("p (j i o) -> p j i o", i=2, o=2).unsqueeze(1).to_broadcast(full),
+                            op=ALU.mult,
+                        )
+                        terms = prod[:].rearrange("p (m i o) -> p m i o", i=2, o=2)
+                        nc.gpsimd.tensor_tensor(
+                            out=res_cols.rearrange("p (m o) -> p m o", o=2),
+                            in0=terms[:, :, 0, :],
+                            in1=terms[:, :, 1, :],
+                            op=ALU.add,
+                        )
+                    else:
+                        nc.scalar.copy(out=res_cols, in_=accs[b][:])
+                nc.sync.dma_start(out=out_dram[t][:, col0 : col0 + width], in_=res[:])

@@ -29,16 +29,24 @@ FREQ_RATIO = ROPE_THETA ** (-1.0 / PAIRS)
 ROUND_MAGIC = 12582912.0
 
 FLOPS = 2 * S * D * (2048 + 512 + 512)
+PROD_BUFS = 8
+VECTOR_ADDS = 3
 
 
-def load_scale_rows(nc, plane, scales_dram, col0, width):
+def load_scale_rows(nc, plane, scales_dram):
     rows = scales_dram.bitcast(I32)
-    for b in range(2):
-        for r in range(4):
-            nc.sync.dma_start(
-                out=plane[32 * b + r : P : 64, :, :].bitcast(I32),
-                in_=rows[:, 4 * b + r : 16 : 8, col0 // 4 : (col0 + width) // 4].rearrange("g q n -> q g n"),
-            )
+    for quad in range(4):
+        nc.sync.dma_start(
+            out=plane[32 * quad : 32 * quad + 4, :, :].bitcast(I32),
+            in_=rows[:, 4 * quad : 4 * quad + 4, :].rearrange("g q n -> q g n"),
+        )
+
+
+def load_words(nc, w_tile, words_dram, col0, width):
+    nc.sync.dma_start(
+        out=w_tile[:].bitcast(I32),
+        in_=words_dram.bitcast(I32)[:, :, col0 // 2 : (col0 + width) // 2].rearrange("g p n -> p g n"),
+    )
 
 
 def tile_rptattention_pa_kernel(
@@ -50,111 +58,118 @@ def tile_rptattention_pa_kernel(
     k_dram = out_1[0].rearrange("(t p) h d -> t p (h d)", p=P)
     v_dram = out_2[0].rearrange("(t p) h d -> t p (h d)", p=P)
 
-    groups = [
-        ("k", wk_words, wk_scales, 0, BANK, k_dram, True),
-        ("q_lo", wq_words, wq_scales, 0, 2 * BANK, q_dram, True),
-        ("q_hi", wq_words, wq_scales, 2 * BANK, 2 * BANK, q_dram, True),
-        ("v", wv_words, wv_scales, 0, BANK, v_dram, False),
-    ]
-
     with ExitStack() as ctx:
         keep = ctx.enter_context(tc.tile_pool(name="keep", bufs=1))
         stage = ctx.enter_context(tc.tile_pool(name="stage", bufs=4))
-        psum_t = ctx.enter_context(tc.psum_pool(name="psum_t", bufs=2))
-        psum_acc = ctx.enter_context(tc.psum_pool(name="psum_acc", bufs=6))
+        prods = ctx.enter_context(tc.tile_pool(name="prods", bufs=PROD_BUFS))
+        psum = ctx.enter_context(tc.psum_pool(name="psum", bufs=8))
+        ctx.enter_context(tc.manual_schedule())
 
-        x_sb = []
-        for t in range(TOK_TILES):
-            x_tile = keep.tile([P, D], BF16, name="x_%d" % t)
-            nc.scalar.dma_start(out=x_tile[:], in_=x_dram[t])
-            x_sb.append(x_tile)
+        plane_k = keep.tile([P, PASSES, BANK], U8, align_bytes=64, name="plane_k")
+        plane_q = keep.tile([P, PASSES, 4 * BANK], U8, align_bytes=64, name="plane_q")
+        plane_v = keep.tile([P, PASSES, BANK], U8, align_bytes=64, name="plane_v")
+        w_k = keep.tile([P, PASSES, 2 * BANK], U8, align_bytes=64, name="w_k")
+        w_q_lo = keep.tile([P, PASSES, 4 * BANK], U8, align_bytes=64, name="w_q_lo")
+        w_q_hi = keep.tile([P, PASSES, 4 * BANK], U8, align_bytes=64, name="w_q_hi")
+        w_v = keep.tile([P, PASSES, 2 * BANK], U8, align_bytes=64, name="w_v")
+        pos_i = keep.tile([P, TOK_TILES], I32, name="pos_i")
+        nc.gpsimd.iota(pos_i[:], pattern=[[P, TOK_TILES]], base=0, channel_multiplier=1)
+        ident = keep.tile([P, P], F32, name="ident")
+        masks.make_identity(nc, ident[:])
+        nc.vector.memset(plane_k[:].rearrange("p g n -> p (g n)").bitcast(I32), 0)
+        for plane in (plane_q, plane_v):
+            nc.gpsimd.memset(plane[:].rearrange("p g n -> p (g n)").bitcast(F32), 0.0)
 
-        w_planes = {}
-        w_words = {}
-        for name, words, scales, col0, width, out_dram, rotated in groups:
-            plane = keep.tile([P, PASSES, width], U8, align_bytes=64, name="plane_%s" % name)
-            nc.vector.memset(plane[:].rearrange("p g n -> p (g n)").bitcast(I32), 0)
-            w_planes[name] = plane
-        for name, words, scales, col0, width, out_dram, rotated in groups:
-            load_scale_rows(nc, w_planes[name], scales, col0, width)
-            words_i32 = words.bitcast(I32)
-            for g in range(PASSES):
-                w_tile = keep.tile([P, 2 * width], U8, align_bytes=64, name="w_%s_%d" % (name, g))
-                nc.sync.dma_start(
-                    out=w_tile[:].bitcast(I32),
-                    in_=words_i32[g, :, col0 // 2 : (col0 + width) // 2],
-                )
-                w_words[(name, g)] = w_tile
+        x_sb = {}
+
+        def load_x(t):
+            for half in range(2):
+                x_half = keep.tile([P, D // 2], BF16, name="x_%d_%d" % (t, half))
+                nc.sync.dma_start(out=x_half[:], in_=x_dram[t][:, half * (D // 2) : (half + 1) * (D // 2)])
+                x_sb[(t, half)] = x_half
+
+        load_x(0)
+        load_scale_rows(nc, plane_k, wk_scales)
+        load_words(nc, w_k, wk_words, 0, BANK)
+        load_x(1)
+        load_x(2)
+        load_x(3)
+        load_words(nc, w_q_lo, wq_words, 0, 2 * BANK)
+        load_scale_rows(nc, plane_q, wq_scales)
+        load_words(nc, w_q_hi, wq_words, 2 * BANK, 2 * BANK)
+        load_words(nc, w_v, wv_words, 0, BANK)
+        load_scale_rows(nc, plane_v, wv_scales)
 
         zero = keep.tile([P, 1], F32, name="zero")
         nc.vector.memset(zero[:], 0.0)
         warm = keep.tile([P, 1], F32, name="warm")
         nc.scalar.activation(out=warm[:], in_=zero[:], func=ACT.Sin)
 
-        ident = keep.tile([P, P], F32, name="ident")
-        masks.make_identity(nc, ident[:])
-
-        pos_i = keep.tile([P, TOK_TILES], I32, name="pos_i")
-        nc.gpsimd.iota(pos_i[:], pattern=[[P, TOK_TILES]], base=0, channel_multiplier=1)
         pos = keep.tile([P, TOK_TILES], F32, name="pos")
         nc.vector.tensor_copy(out=pos[:], in_=pos_i[:])
-
-        turns = keep.tile([P, PAIRS, 4], F32, name="turns")
-        nc.vector.memset(turns[:, 0:1, :], 1.0)
+        freq = keep.tile([P, 3, PAIRS], F32, name="freq")
+        nc.vector.memset(freq[:, :, 0:1], 1.0)
         nc.vector.tensor_scalar(
-            out=turns[:, 0:1, :], in0=turns[:, 0:1, :], scalar1=1.0 / (2.0 * math.pi), scalar2=None, op0=ALU.mult
+            out=freq[:, :, 0:1], in0=freq[:, :, 0:1], scalar1=1.0 / (2.0 * math.pi), scalar2=None, op0=ALU.mult
         )
         for step in range(6):
             have = 2**step
             nc.vector.tensor_scalar(
-                out=turns[:, have : 2 * have, :],
-                in0=turns[:, 0:have, :],
+                out=freq[:, :, have : 2 * have],
+                in0=freq[:, :, 0:have],
                 scalar1=FREQ_RATIO**have,
                 scalar2=None,
                 op0=ALU.mult,
             )
-        phase = keep.tile([P, PAIRS, 2, 2], F32, name="phase")
-        nc.vector.memset(phase[:], 0.25)
-        nc.vector.memset(phase[:, :, 0, 1], 0.0)
-        nc.vector.memset(phase[:, :, 1, 0], 0.5)
-
-        rot = []
+        phase = keep.tile([P, 3, PAIRS], F32, name="phase")
+        nc.vector.memset(phase[:, 0, :], 0.5)
+        nc.vector.memset(phase[:, 1, :], 0.25)
+        nc.vector.memset(phase[:, 2, :], 0.0)
+        angle = keep.tile([P, TOK_TILES, 3 * PAIRS], F32, name="angle")
         for t in range(TOK_TILES):
-            angle = stage.tile([P, 4 * PAIRS], F32, name="angle")
             nc.vector.scalar_tensor_tensor(
-                out=angle[:],
-                in0=turns[:].rearrange("p j c -> p (j c)"),
+                out=angle[:, t, :],
+                in0=freq[:].rearrange("p c j -> p (c j)"),
                 scalar=pos[:, t : t + 1],
-                in1=phase[:].rearrange("p j i o -> p (j i o)"),
+                in1=phase[:].rearrange("p c j -> p (c j)"),
                 op0=ALU.mult,
                 op1=ALU.add,
             )
-            shifted = stage.tile([P, 4 * PAIRS], F32, name="shifted")
-            nc.vector.tensor_scalar(out=shifted[:], in0=angle[:], scalar1=ROUND_MAGIC, scalar2=None, op0=ALU.add)
-            neg_frac = stage.tile([P, 4 * PAIRS], F32, name="neg_frac")
-            nc.vector.scalar_tensor_tensor(
-                out=neg_frac[:],
-                in0=shifted[:],
-                scalar=ROUND_MAGIC,
-                in1=angle[:],
-                op0=ALU.subtract,
-                op1=ALU.subtract,
-            )
-            rot_t = keep.tile([P, 4 * PAIRS], F32, name="rot_%d" % t)
-            nc.scalar.activation(out=rot_t[:], in_=neg_frac[:], func=ACT.Sin, scale=-2.0 * math.pi)
-            rot.append(rot_t)
+        shifted = keep.tile([P, TOK_TILES * 3 * PAIRS], F32, name="shifted")
+        nc.vector.tensor_scalar(
+            out=shifted[:], in0=angle[:].rearrange("p t c -> p (t c)"), scalar1=ROUND_MAGIC, scalar2=None, op0=ALU.add
+        )
+        neg_frac = keep.tile([P, TOK_TILES, 3, PAIRS], F32, name="neg_frac")
+        nc.vector.scalar_tensor_tensor(
+            out=neg_frac[:].rearrange("p t c j -> p (t c j)"),
+            in0=shifted[:],
+            scalar=ROUND_MAGIC,
+            in1=angle[:].rearrange("p t c -> p (t c)"),
+            op0=ALU.subtract,
+            op1=ALU.subtract,
+        )
+        rot_all = keep.tile([P, TOK_TILES, 2, PAIRS, 2], F32, name="rot_all")
+
+        def make_factors():
+            for i in range(2):
+                nc.scalar.activation(
+                    out=rot_all[:, :, i, :, :],
+                    in_=neg_frac[:, :, 1 - i : 3 - i, :].rearrange("p t c j -> p t j c"),
+                    func=ACT.Sin,
+                    scale=-2.0 * math.pi,
+                )
 
         x_codes = {}
         x_scales = {}
-        for t in range(TOK_TILES):
-            x_words = x_sb[t][:].bitcast(F32)
+
+        def quantise_x(t):
             for half in range(2):
-                xt = psum_t.tile([P, 2, 2, P], F32, name="xt")
+                x_words = x_sb[(t, half)][:].bitcast(F32)
+                xt = psum.tile([P, 2, 2, P], F32, name="xt", tag="bank")
                 for gg in range(2):
-                    g = 2 * half + gg
                     for u in range(2):
                         nc.tensor.transpose(
-                            xt[:, gg, u, :], x_words[:, 256 * g + u : 256 * (g + 1) : 2], ident[:]
+                            xt[:, gg, u, :], x_words[:, 256 * gg + u : 256 * (gg + 1) : 2], ident[:]
                         )
                 grouped = stage.tile([P, 2 * P * 4], BF16, align_bytes=64, name="grouped")
                 nc.scalar.copy(
@@ -168,46 +183,71 @@ def tile_rptattention_pa_kernel(
                     x_codes[(t, 2 * half + gg)] = codes[:, gg * P : (gg + 1) * P]
                     x_scales[(t, 2 * half + gg)] = scales[:, gg * P : (gg + 1) * P]
 
-        for name, words, scales, col0, width, out_dram, rotated in groups:
-            banks = width // BANK
-            for t in range(TOK_TILES):
-                accs = []
-                for b in range(banks):
-                    acc = psum_acc.tile([P, BANK], F32, name="acc")
-                    accs.append(acc)
-                for g in range(PASSES):
-                    for b in range(banks):
-                        nc.tensor.matmul_mx(
-                            out=accs[b][:],
-                            lhsT=x_codes[(t, g)].bitcast(FP8X4),
-                            lhsT_scale=x_scales[(t, g)],
-                            rhs=w_words[(name, g)][:, 2 * BANK * b : 2 * BANK * (b + 1)].bitcast(FP4X4),
-                            rhs_scale=w_planes[name][:, g, BANK * b : BANK * (b + 1)],
-                            start=(g == 0),
-                            stop=(g == PASSES - 1),
-                        )
-                res = keep.tile([P, width], F32, name="res_%s_%d" % (name, t))
-                for b in range(banks):
+        def bank_sums(t, w_tile, w_col0, plane, plane_col0):
+            acc = psum.tile([P, BANK], F32, name="acc", tag="bank")
+            for g in range(PASSES):
+                nc.tensor.matmul_mx(
+                    out=acc[:],
+                    lhsT=x_codes[(t, g)].bitcast(FP8X4),
+                    lhsT_scale=x_scales[(t, g)],
+                    rhs=w_tile[:, g, 2 * w_col0 : 2 * (w_col0 + BANK)].bitcast(FP4X4),
+                    rhs_scale=plane[:, g, plane_col0 : plane_col0 + BANK],
+                    start=(g == 0),
+                    stop=(g == PASSES - 1),
+                )
+            return acc
+
+        def rotate(t, acc, res_cols, add_engine):
+            prod = prods.tile([P, 2, BANK], F32, name="prod")
+            full = [P, 2, HEADS_PER_BANK, PAIRS, 2]
+            nc.vector.tensor_tensor(
+                out=prod[:].rearrange("p i (h j o) -> p i h j o", h=HEADS_PER_BANK, o=2),
+                in0=acc[:].rearrange("p (h j i) -> p i h j", h=HEADS_PER_BANK, i=2).unsqueeze(4).to_broadcast(full),
+                in1=rot_all[:, t].unsqueeze(2).to_broadcast(full),
+                op=ALU.mult,
+            )
+            return lambda: add_engine.tensor_tensor(out=res_cols, in0=prod[:, 0, :], in1=prod[:, 1, :], op=ALU.add)
+
+        def k_bank(t):
+            acc = bank_sums(t, w_k, 0, plane_k, 0)
+            res = keep.tile([P, BANK], F32, name="res_k_%d" % t)
+            rotate(t, acc, res[:], nc.gpsimd)()
+            nc.sync.dma_start(out=k_dram[t], in_=res[:])
+
+        quantise_x(0)
+        make_factors()
+        k_bank(0)
+        quantise_x(1)
+        quantise_x(2)
+        k_bank(1)
+        quantise_x(3)
+        k_bank(2)
+        k_bank(3)
+
+        late_adds = []
+        for t in range(TOK_TILES):
+            for w_tile, col0 in ((w_q_lo, 0), (w_q_hi, 2 * BANK)):
+                res = keep.tile([P, 2 * BANK], F32, name="res_q_%d_%d" % (t, col0))
+                for b in range(2):
+                    acc = bank_sums(t, w_tile, BANK * b, plane_q, col0 + BANK * b)
                     res_cols = res[:, BANK * b : BANK * (b + 1)]
-                    if rotated:
-                        prod = stage.tile([P, 2 * BANK], F32, name="prod")
-                        full = [P, HEADS_PER_BANK, PAIRS, 2, 2]
-                        nc.vector.tensor_tensor(
-                            out=prod[:].rearrange("p (h j i o) -> p h j i o", h=HEADS_PER_BANK, i=2, o=2),
-                            in0=accs[b][:]
-                            .rearrange("p (h j i) -> p h j i", h=HEADS_PER_BANK, i=2)
-                            .unsqueeze(4)
-                            .to_broadcast(full),
-                            in1=rot[t][:].rearrange("p (j i o) -> p j i o", i=2, o=2).unsqueeze(1).to_broadcast(full),
-                            op=ALU.mult,
-                        )
-                        terms = prod[:].rearrange("p (m i o) -> p m i o", i=2, o=2)
-                        nc.gpsimd.tensor_tensor(
-                            out=res_cols.rearrange("p (m o) -> p m o", o=2),
-                            in0=terms[:, :, 0, :],
-                            in1=terms[:, :, 1, :],
-                            op=ALU.add,
-                        )
+                    out_cols = q_dram[t][:, col0 + BANK * b : col0 + BANK * (b + 1)]
+                    on_vector = 4 * t + col0 // BANK + b >= 4 * TOK_TILES - VECTOR_ADDS
+                    add = rotate(t, acc, res_cols, nc.vector if on_vector else nc.gpsimd)
+                    if on_vector:
+                        late_adds.append((add, out_cols, res_cols))
                     else:
-                        nc.scalar.copy(out=res_cols, in_=accs[b][:])
-                nc.sync.dma_start(out=out_dram[t][:, col0 : col0 + width], in_=res[:])
+                        add()
+                        if t == TOK_TILES - 1:
+                            nc.sync.dma_start(out=out_cols, in_=res_cols)
+                if t < TOK_TILES - 1:
+                    nc.sync.dma_start(out=q_dram[t][:, col0 : col0 + 2 * BANK], in_=res[:])
+        for add, out_cols, res_cols in late_adds:
+            add()
+            nc.sync.dma_start(out=out_cols, in_=res_cols)
+
+        for t in range(TOK_TILES):
+            acc = bank_sums(t, w_v, 0, plane_v, 0)
+            res = keep.tile([P, BANK], F32, name="res_v_%d" % t)
+            nc.scalar.copy(out=res[:], in_=acc[:])
+            nc.sync.dma_start(out=v_dram[t], in_=res[:])

@@ -76,9 +76,8 @@ def tile_rptattention_pa_kernel(
         nc.gpsimd.iota(pos_i[:], pattern=[[P, TOK_TILES]], base=0, channel_multiplier=1)
         ident = keep.tile([P, P], F32, name="ident")
         masks.make_identity(nc, ident[:])
-        nc.vector.memset(plane_k[:].rearrange("p g n -> p (g n)").bitcast(I32), 0)
-        for plane in (plane_q, plane_v):
-            nc.gpsimd.memset(plane[:].rearrange("p g n -> p (g n)").bitcast(F32), 0.0)
+        for plane in (plane_k, plane_q, plane_v):
+            nc.vector.memset(plane[:].rearrange("p g n -> p (g n)").bitcast(I32), 0)
 
         x_sb = {}
 

@@ -76,8 +76,7 @@ def tile_rptattention_pa_kernel(
         nc.gpsimd.iota(pos_i[:], pattern=[[P, TOK_TILES]], base=0, channel_multiplier=1)
         ident = keep.tile([P, P], F32, name="ident")
         masks.make_identity(nc, ident[:])
-        for plane in (plane_k, plane_q, plane_v):
-            nc.vector.memset(plane[:].rearrange("p g n -> p (g n)").bitcast(I32), 0)
+        nc.vector.memset(plane_k[:].rearrange("p g n -> p (g n)").bitcast(I32), 0)
 
         x_sb = {}
 
@@ -94,10 +93,6 @@ def tile_rptattention_pa_kernel(
         load_x(2)
         load_x(3)
         load_words(nc, w_q_lo, wq_words, 0, 2 * BANK)
-        load_scale_rows(nc, plane_q, wq_scales)
-        load_words(nc, w_q_hi, wq_words, 2 * BANK, 2 * BANK)
-        load_words(nc, w_v, wv_words, 0, BANK)
-        load_scale_rows(nc, plane_v, wv_scales)
 
         zero = keep.tile([P, 1], F32, name="zero")
         nc.vector.memset(zero[:], 0.0)
@@ -214,6 +209,12 @@ def tile_rptattention_pa_kernel(
             nc.sync.dma_start(out=k_dram[t], in_=res[:])
 
         quantise_x(0)
+        for plane in (plane_q, plane_v):
+            nc.vector.memset(plane[:].rearrange("p g n -> p (g n)").bitcast(I32), 0)
+        load_scale_rows(nc, plane_q, wq_scales)
+        load_words(nc, w_q_hi, wq_words, 2 * BANK, 2 * BANK)
+        load_words(nc, w_v, wv_words, 0, BANK)
+        load_scale_rows(nc, plane_v, wv_scales)
         make_factors()
         k_bank(0)
         quantise_x(1)

@@ -72,8 +72,10 @@ def tile_rptattention_pa_kernel(
         w_q_lo = keep.tile([P, PASSES, 4 * BANK], U8, align_bytes=64, name="w_q_lo")
         w_q_hi = keep.tile([P, PASSES, 4 * BANK], U8, align_bytes=64, name="w_q_hi")
         w_v = keep.tile([P, PASSES, 2 * BANK], U8, align_bytes=64, name="w_v")
-        pos_i = keep.tile([P, TOK_TILES], I32, name="pos_i")
-        nc.gpsimd.iota(pos_i[:], pattern=[[P, TOK_TILES]], base=0, channel_multiplier=1)
+        pos = keep.tile([P, TOK_TILES], F32, name="pos")
+        nc.gpsimd.iota(
+            pos[:], pattern=[[P, TOK_TILES]], base=0, channel_multiplier=1, allow_small_or_imprecise_dtypes=True
+        )
         ident = keep.tile([P, P], F32, name="ident")
         masks.make_identity(nc, ident[:])
         nc.vector.memset(plane_k[:].rearrange("p g n -> p (g n)").bitcast(I32), 0)
@@ -94,38 +96,34 @@ def tile_rptattention_pa_kernel(
         load_x(3)
         load_words(nc, w_q_lo, wq_words, 0, 2 * BANK)
 
-        zero = keep.tile([P, 1], F32, name="zero")
-        nc.vector.memset(zero[:], 0.0)
+        ones = keep.tile([P, PAIRS], F32, name="ones")
+        nc.vector.memset(ones[:], 1.0)
+        nought = keep.tile([P, PAIRS], F32, name="nought")
+        nc.vector.memset(nought[:], 0.0)
         warm = keep.tile([P, 1], F32, name="warm")
-        nc.scalar.activation(out=warm[:], in_=zero[:], func=ACT.Sin)
-
-        pos = keep.tile([P, TOK_TILES], F32, name="pos")
-        nc.vector.tensor_copy(out=pos[:], in_=pos_i[:])
-        freq = keep.tile([P, 3, PAIRS], F32, name="freq")
-        nc.vector.memset(freq[:, :, 0:1], 1.0)
-        nc.vector.tensor_scalar(
-            out=freq[:, :, 0:1], in0=freq[:, :, 0:1], scalar1=1.0 / (2.0 * math.pi), scalar2=None, op0=ALU.mult
-        )
-        for step in range(6):
-            have = 2**step
-            nc.vector.tensor_scalar(
-                out=freq[:, :, have : 2 * have],
-                in0=freq[:, :, 0:have],
-                scalar1=FREQ_RATIO**have,
-                scalar2=None,
-                op0=ALU.mult,
-            )
+        nc.scalar.activation(out=warm[:], in_=nought[:, 0:1], func=ACT.Sin)
+        ratio = keep.tile([P, PAIRS], F32, name="ratio")
+        nc.vector.tensor_scalar(out=ratio[:], in0=ones[:], scalar1=FREQ_RATIO, scalar2=None, op0=ALU.mult)
         phase = keep.tile([P, 3, PAIRS], F32, name="phase")
         nc.vector.memset(phase[:, 0, :], 0.5)
         nc.vector.memset(phase[:, 1, :], 0.25)
         nc.vector.memset(phase[:, 2, :], 0.0)
+        freq = keep.tile([P, PAIRS], F32, name="freq")
+        nc.vector.tensor_tensor_scan(
+            out=freq[:],
+            data0=ratio[:],
+            data1=nought[:],
+            initial=1.0 / (2.0 * math.pi * FREQ_RATIO),
+            op0=ALU.mult,
+            op1=ALU.add,
+        )
         angle = keep.tile([P, TOK_TILES, 3 * PAIRS], F32, name="angle")
         for t in range(TOK_TILES):
             nc.vector.scalar_tensor_tensor(
-                out=angle[:, t, :],
-                in0=freq[:].rearrange("p c j -> p (c j)"),
+                out=angle[:, t, :].rearrange("p (c j) -> p c j", c=3),
+                in0=freq[:].unsqueeze(1).to_broadcast([P, 3, PAIRS]),
                 scalar=pos[:, t : t + 1],
-                in1=phase[:].rearrange("p c j -> p (c j)"),
+                in1=phase[:],
                 op0=ALU.mult,
                 op1=ALU.add,
             )

@@ -104,10 +104,6 @@ def tile_rptattention_pa_kernel(
         nc.scalar.activation(out=warm[:], in_=nought[:, 0:1], func=ACT.Sin)
         ratio = keep.tile([P, PAIRS], F32, name="ratio")
         nc.vector.tensor_scalar(out=ratio[:], in0=ones[:], scalar1=FREQ_RATIO, scalar2=None, op0=ALU.mult)
-        phase = keep.tile([P, 3, PAIRS], F32, name="phase")
-        nc.vector.memset(phase[:, 0, :], 0.5)
-        nc.vector.memset(phase[:, 1, :], 0.25)
-        nc.vector.memset(phase[:, 2, :], 0.0)
         freq = keep.tile([P, PAIRS], F32, name="freq")
         nc.vector.tensor_tensor_scan(
             out=freq[:],
@@ -117,38 +113,39 @@ def tile_rptattention_pa_kernel(
             op0=ALU.mult,
             op1=ALU.add,
         )
-        angle = keep.tile([P, TOK_TILES, 3 * PAIRS], F32, name="angle")
-        for t in range(TOK_TILES):
-            nc.vector.scalar_tensor_tensor(
-                out=angle[:, t, :].rearrange("p (c j) -> p c j", c=3),
-                in0=freq[:].unsqueeze(1).to_broadcast([P, 3, PAIRS]),
-                scalar=pos[:, t : t + 1],
-                in1=phase[:],
-                op0=ALU.mult,
-                op1=ALU.add,
-            )
-        shifted = keep.tile([P, TOK_TILES * 3 * PAIRS], F32, name="shifted")
-        nc.vector.tensor_scalar(
-            out=shifted[:], in0=angle[:].rearrange("p t c -> p (t c)"), scalar1=ROUND_MAGIC, scalar2=None, op0=ALU.add
+        angle = keep.tile([P, TOK_TILES, PAIRS], F32, name="angle")
+        nc.vector.tensor_tensor(
+            out=angle[:],
+            in0=freq[:].unsqueeze(1).to_broadcast([P, TOK_TILES, PAIRS]),
+            in1=pos[:].unsqueeze(2).to_broadcast([P, TOK_TILES, PAIRS]),
+            op=ALU.mult,
         )
-        neg_frac = keep.tile([P, TOK_TILES, 3, PAIRS], F32, name="neg_frac")
+        shifted = keep.tile([P, TOK_TILES, PAIRS], F32, name="shifted")
+        nc.vector.tensor_scalar(out=shifted[:], in0=angle[:], scalar1=ROUND_MAGIC, scalar2=None, op0=ALU.add)
+        turn = keep.tile([P, TOK_TILES, 3, PAIRS], F32, name="turn")
         nc.vector.scalar_tensor_tensor(
-            out=neg_frac[:].rearrange("p t c j -> p (t c j)"),
+            out=turn[:, :, 0, :],
             in0=shifted[:],
             scalar=ROUND_MAGIC,
-            in1=angle[:].rearrange("p t c -> p (t c)"),
+            in1=angle[:],
             op0=ALU.subtract,
             op1=ALU.subtract,
         )
+        size = keep.tile([P, TOK_TILES, PAIRS], F32, name="size")
         rot_all = keep.tile([P, TOK_TILES, 2, PAIRS, 2], F32, name="rot_all")
+
+        def make_turns():
+            nc.scalar.activation(out=size[:], in_=turn[:, :, 0, :], func=ACT.Abs)
+            nc.scalar.activation(out=turn[:, :, 1, :], in_=size[:], func=ACT.Copy, scale=-1.0, bias=0.25)
+            nc.scalar.activation(out=turn[:, :, 2, :], in_=turn[:, :, 0, :], func=ACT.Copy, scale=-1.0)
 
         def make_factors():
             for i in range(2):
                 nc.scalar.activation(
                     out=rot_all[:, :, i, :, :],
-                    in_=neg_frac[:, :, 1 - i : 3 - i, :].rearrange("p t c j -> p t j c"),
+                    in_=turn[:, :, 1 - i : 3 - i, :].rearrange("p t c j -> p t j c"),
                     func=ACT.Sin,
-                    scale=-2.0 * math.pi,
+                    scale=2.0 * math.pi,
                 )
 
         x_codes = {}
@@ -213,6 +210,7 @@ def tile_rptattention_pa_kernel(
         load_words(nc, w_q_hi, wq_words, 2 * BANK, 2 * BANK)
         load_words(nc, w_v, wv_words, 0, BANK)
         load_scale_rows(nc, plane_v, wv_scales)
+        make_turns()
         make_factors()
         k_bank(0)
         quantise_x(1)

@@ -33,12 +33,12 @@ PROD_BUFS = 8
 VECTOR_ADDS = 3
 
 
-def load_scale_rows(nc, plane, scales_dram):
+def load_scale_rows(nc, plane, scales_dram, col0, width):
     rows = scales_dram.bitcast(I32)
     for quad in range(4):
         nc.sync.dma_start(
             out=plane[32 * quad : 32 * quad + 4, :, :].bitcast(I32),
-            in_=rows[:, 4 * quad : 4 * quad + 4, :].rearrange("g q n -> q g n"),
+            in_=rows[:, 4 * quad : 4 * quad + 4, col0 // 4 : (col0 + width) // 4].rearrange("g q n -> q g n"),
         )
 
 
@@ -66,7 +66,8 @@ def tile_rptattention_pa_kernel(
         ctx.enter_context(tc.manual_schedule())
 
         plane_k = keep.tile([P, PASSES, BANK], U8, align_bytes=64, name="plane_k")
-        plane_q = keep.tile([P, PASSES, 4 * BANK], U8, align_bytes=64, name="plane_q")
+        plane_q_lo = keep.tile([P, PASSES, 2 * BANK], U8, align_bytes=64, name="plane_q_lo")
+        plane_q_hi = keep.tile([P, PASSES, 2 * BANK], U8, align_bytes=64, name="plane_q_hi")
         plane_v = keep.tile([P, PASSES, BANK], U8, align_bytes=64, name="plane_v")
         w_k = keep.tile([P, PASSES, 2 * BANK], U8, align_bytes=64, name="w_k")
         w_q_lo = keep.tile([P, PASSES, 4 * BANK], U8, align_bytes=64, name="w_q_lo")
@@ -89,7 +90,7 @@ def tile_rptattention_pa_kernel(
                 x_sb[(t, half)] = x_half
 
         load_x(0)
-        load_scale_rows(nc, plane_k, wk_scales)
+        load_scale_rows(nc, plane_k, wk_scales, 0, BANK)
         load_words(nc, w_k, wk_words, 0, BANK)
         load_x(1)
         load_x(2)
@@ -204,12 +205,13 @@ def tile_rptattention_pa_kernel(
             nc.sync.dma_start(out=k_dram[t], in_=res[:])
 
         quantise_x(0)
-        for plane in (plane_q, plane_v):
+        for plane in (plane_q_lo, plane_q_hi, plane_v):
             nc.vector.memset(plane[:].rearrange("p g n -> p (g n)").bitcast(I32), 0)
-        load_scale_rows(nc, plane_q, wq_scales)
+        load_scale_rows(nc, plane_q_lo, wq_scales, 0, 2 * BANK)
         load_words(nc, w_q_hi, wq_words, 2 * BANK, 2 * BANK)
+        load_scale_rows(nc, plane_q_hi, wq_scales, 2 * BANK, 2 * BANK)
         load_words(nc, w_v, wv_words, 0, BANK)
-        load_scale_rows(nc, plane_v, wv_scales)
+        load_scale_rows(nc, plane_v, wv_scales, 0, BANK)
         make_turns()
         make_factors()
         k_bank(0)
@@ -221,22 +223,25 @@ def tile_rptattention_pa_kernel(
         k_bank(3)
 
         late_adds = []
-        for t in range(TOK_TILES):
-            for w_tile, col0 in ((w_q_lo, 0), (w_q_hi, 2 * BANK)):
+        banks_done = 0
+        for w_tile, plane, col0 in ((w_q_lo, plane_q_lo, 0), (w_q_hi, plane_q_hi, 2 * BANK)):
+            for t in range(TOK_TILES):
+                at_the_end = col0 > 0 and t >= TOK_TILES - 2
                 res = keep.tile([P, 2 * BANK], F32, name="res_q_%d_%d" % (t, col0))
                 for b in range(2):
-                    acc = bank_sums(t, w_tile, BANK * b, plane_q, col0 + BANK * b)
+                    acc = bank_sums(t, w_tile, BANK * b, plane, BANK * b)
                     res_cols = res[:, BANK * b : BANK * (b + 1)]
                     out_cols = q_dram[t][:, col0 + BANK * b : col0 + BANK * (b + 1)]
-                    on_vector = 4 * t + col0 // BANK + b >= 4 * TOK_TILES - VECTOR_ADDS
+                    on_vector = banks_done >= 4 * TOK_TILES - VECTOR_ADDS
+                    banks_done += 1
                     add = rotate(t, acc, res_cols, nc.vector if on_vector else nc.gpsimd)
                     if on_vector:
                         late_adds.append((add, out_cols, res_cols))
                     else:
                         add()
-                        if t == TOK_TILES - 1:
+                        if at_the_end:
                             nc.sync.dma_start(out=out_cols, in_=res_cols)
-                if t < TOK_TILES - 1:
+                if not at_the_end:
                     nc.sync.dma_start(out=q_dram[t][:, col0 : col0 + 2 * BANK], in_=res[:])
         for add, out_cols, res_cols in late_adds:
             add()

@@ -60,7 +60,6 @@ def tile_rptattention_pa_kernel(
 
     with ExitStack() as ctx:
         keep = ctx.enter_context(tc.tile_pool(name="keep", bufs=1))
-        stage = ctx.enter_context(tc.tile_pool(name="stage", bufs=4))
         prods = ctx.enter_context(tc.tile_pool(name="prods", bufs=PROD_BUFS))
         psum = ctx.enter_context(tc.psum_pool(name="psum", bufs=8))
         ctx.enter_context(tc.manual_schedule())
@@ -90,9 +89,9 @@ def tile_rptattention_pa_kernel(
                 x_sb[(t, half)] = x_half
 
         load_x(0)
+        load_x(1)
         load_scale_rows(nc, plane_k, wk_scales, 0, BANK)
         load_words(nc, w_k, wk_words, 0, BANK)
-        load_x(1)
         load_x(2)
         load_x(3)
         load_words(nc, w_q_lo, wq_words, 0, 2 * BANK)
@@ -152,23 +151,41 @@ def tile_rptattention_pa_kernel(
         x_codes = {}
         x_scales = {}
 
-        def quantise_x(t):
+        x_sorted = {}
+        x_grouped = {}
+
+        def sort_x(t):
             for half in range(2):
-                x_words = x_sb[(t, half)][:].bitcast(F32)
+                ordered = keep.tile([P, D // 4], F32, name="x_sorted_%d_%d" % (t, half))
+                nc.vector.tensor_copy(
+                    out=ordered[:].rearrange("p (g u w) -> p g u w", g=2, u=2),
+                    in_=x_sb[(t, half)][:].bitcast(F32).rearrange("p (g w u) -> p g u w", g=2, u=2),
+                )
+                x_sorted[(t, half)] = ordered
+
+        def turn_x(t):
+            for half in range(2):
                 xt = psum.tile([P, 2, 2, P], F32, name="xt", tag="bank")
                 for gg in range(2):
                     for u in range(2):
-                        nc.tensor.transpose(
-                            xt[:, gg, u, :], x_words[:, 256 * gg + u : 256 * (gg + 1) : 2], ident[:]
-                        )
-                grouped = stage.tile([P, 2 * P * 4], BF16, align_bytes=64, name="grouped")
+                        if (t, half) in x_sorted:
+                            col0 = (2 * gg + u) * P
+                            words = x_sorted[(t, half)][:, col0 : col0 + P]
+                        else:
+                            words = x_sb[(t, half)][:].bitcast(F32)[:, 256 * gg + u : 256 * (gg + 1) : 2]
+                        nc.tensor.transpose(xt[:, gg, u, :], words, ident[:])
+                grouped = keep.tile([P, 2 * P * 4], BF16, align_bytes=64, name="grouped_%d_%d" % (t, half))
                 nc.scalar.copy(
                     out=grouped[:].bitcast(F32).rearrange("p (g r u) -> p g r u", g=2, u=2),
                     in_=xt[:].rearrange("p g u r -> p g r u"),
                 )
+                x_grouped[(t, half)] = grouped
+
+        def quant_x(t):
+            for half in range(2):
                 codes = keep.tile([P, 2 * P], U32, align_bytes=64, name="x_codes_%d_%d" % (t, half))
                 scales = keep.tile([P, 2 * P], U8, align_bytes=64, name="x_scales_%d_%d" % (t, half))
-                nc.vector.quantize_mx(out=codes[:].bitcast(FP8X4), scales=scales[:], in_=grouped[:])
+                nc.vector.quantize_mx(out=codes[:].bitcast(FP8X4), scales=scales[:], in_=x_grouped[(t, half)][:])
                 for gg in range(2):
                     x_codes[(t, 2 * half + gg)] = codes[:, gg * P : (gg + 1) * P]
                     x_scales[(t, 2 * half + gg)] = scales[:, gg * P : (gg + 1) * P]
@@ -204,21 +221,32 @@ def tile_rptattention_pa_kernel(
             rotate(t, acc, res[:], nc.gpsimd)()
             nc.sync.dma_start(out=k_dram[t], in_=res[:])
 
-        quantise_x(0)
-        for plane in (plane_q_lo, plane_q_hi, plane_v):
+        def zero_plane(plane):
             nc.vector.memset(plane[:].rearrange("p g n -> p (g n)").bitcast(I32), 0)
+
+        turn_x(0)
+        sort_x(1)
+        quant_x(0)
+        turn_x(1)
+        zero_plane(plane_q_lo)
         load_scale_rows(nc, plane_q_lo, wq_scales, 0, 2 * BANK)
         load_words(nc, w_q_hi, wq_words, 2 * BANK, 2 * BANK)
-        load_scale_rows(nc, plane_q_hi, wq_scales, 2 * BANK, 2 * BANK)
         load_words(nc, w_v, wv_words, 0, BANK)
-        load_scale_rows(nc, plane_v, wv_scales, 0, BANK)
+        quant_x(1)
+        sort_x(2)
+        sort_x(3)
         make_turns()
         make_factors()
         k_bank(0)
-        quantise_x(1)
-        quantise_x(2)
+        turn_x(2)
+        turn_x(3)
+        quant_x(2)
+        quant_x(3)
         k_bank(1)
-        quantise_x(3)
+        zero_plane(plane_q_hi)
+        zero_plane(plane_v)
+        load_scale_rows(nc, plane_q_hi, wq_scales, 2 * BANK, 2 * BANK)
+        load_scale_rows(nc, plane_v, wv_scales, 0, BANK)
         k_bank(2)
         k_bank(3)
 

@@ -66,10 +66,8 @@ def tile_rptattention_pa_kernel(
 
         plane_k = keep.tile([P, PASSES, BANK], U8, align_bytes=64, name="plane_k")
         plane_q_lo = keep.tile([P, PASSES, 2 * BANK], U8, align_bytes=64, name="plane_q_lo")
-        plane_q_hi = keep.tile([P, PASSES, 2 * BANK], U8, align_bytes=64, name="plane_q_hi")
-        plane_v = keep.tile([P, PASSES, BANK], U8, align_bytes=64, name="plane_v")
-        w_k = keep.tile([P, PASSES, 2 * BANK], U8, align_bytes=64, name="w_k")
-        w_q_lo = keep.tile([P, PASSES, 4 * BANK], U8, align_bytes=64, name="w_q_lo")
+        w_k = keep.tile([P, PASSES, 2 * BANK], U8, align_bytes=64, name="w_k", tag="k_words_then_q_plane")
+        w_q_lo = keep.tile([P, PASSES, 4 * BANK], U8, align_bytes=64, name="w_q_lo", tag="q_words_then_v_plane")
         w_q_hi = keep.tile([P, PASSES, 4 * BANK], U8, align_bytes=64, name="w_q_hi")
         w_v = keep.tile([P, PASSES, 2 * BANK], U8, align_bytes=64, name="w_v")
         pos = keep.tile([P, TOK_TILES], F32, name="pos")
@@ -243,12 +241,10 @@ def tile_rptattention_pa_kernel(
         quant_x(2)
         quant_x(3)
         k_bank(1)
-        zero_plane(plane_q_hi)
-        zero_plane(plane_v)
-        load_scale_rows(nc, plane_q_hi, wq_scales, 2 * BANK, 2 * BANK)
-        load_scale_rows(nc, plane_v, wv_scales, 0, BANK)
         k_bank(2)
         k_bank(3)
+        plane_q_hi = keep.tile([P, PASSES, 2 * BANK], U8, align_bytes=64, name="plane_q_hi", tag="k_words_then_q_plane")
+        load_scale_rows(nc, plane_q_hi, wq_scales, 2 * BANK, 2 * BANK)
 
         late_adds = []
         banks_done = 0
@@ -271,6 +267,9 @@ def tile_rptattention_pa_kernel(
                             nc.sync.dma_start(out=out_cols, in_=res_cols)
                 if not at_the_end:
                     nc.sync.dma_start(out=q_dram[t][:, col0 : col0 + 2 * BANK], in_=res[:])
+            if col0 == 0:
+                plane_v = keep.tile([P, PASSES, BANK], U8, align_bytes=64, name="plane_v", tag="q_words_then_v_plane")
+                load_scale_rows(nc, plane_v, wv_scales, 0, BANK)
         for add, out_cols, res_cols in late_adds:
             add()
             nc.sync.dma_start(out=out_cols, in_=res_cols)

@@ -88,10 +88,10 @@ def tile_rptattention_pa_kernel(
 
         load_x(0)
         load_x(1)
-        load_scale_rows(nc, plane_k, wk_scales, 0, BANK)
-        load_words(nc, w_k, wk_words, 0, BANK)
         load_x(2)
         load_x(3)
+        load_scale_rows(nc, plane_k, wk_scales, 0, BANK)
+        load_words(nc, w_k, wk_words, 0, BANK)
         load_words(nc, w_q_lo, wq_words, 0, 2 * BANK)
 
         ones = keep.tile([P, PAIRS], F32, name="ones")
@@ -149,44 +149,30 @@ def tile_rptattention_pa_kernel(
         x_codes = {}
         x_scales = {}
 
-        x_sorted = {}
         x_grouped = {}
 
-        def sort_x(t):
-            for half in range(2):
-                ordered = keep.tile([P, D // 4], F32, name="x_sorted_%d_%d" % (t, half))
-                nc.vector.tensor_copy(
-                    out=ordered[:].rearrange("p (g u w) -> p g u w", g=2, u=2),
-                    in_=x_sb[(t, half)][:].bitcast(F32).rearrange("p (g w u) -> p g u w", g=2, u=2),
-                )
-                x_sorted[(t, half)] = ordered
+        def turn_half(t, half, on_vector=False):
+            xt = psum.tile([P, 2, 2, P], F32, name="xt", tag="bank")
+            for gg in range(2):
+                for u in range(2):
+                    words = x_sb[(t, half)][:].bitcast(F32)[:, 256 * gg + u : 256 * (gg + 1) : 2]
+                    nc.tensor.transpose(xt[:, gg, u, :], words, ident[:])
+            grouped = keep.tile([P, 2 * P * 4], BF16, align_bytes=64, name="grouped_%d_%d" % (t, half))
+            out_words = grouped[:].bitcast(F32).rearrange("p (g r u) -> p g r u", g=2, u=2)
+            in_words = xt[:].rearrange("p g u r -> p g r u")
+            if on_vector:
+                nc.vector.tensor_copy(out=out_words, in_=in_words)
+            else:
+                nc.scalar.copy(out=out_words, in_=in_words)
+            x_grouped[(t, half)] = grouped
 
-        def turn_x(t):
-            for half in range(2):
-                xt = psum.tile([P, 2, 2, P], F32, name="xt", tag="bank")
-                for gg in range(2):
-                    for u in range(2):
-                        if (t, half) in x_sorted:
-                            col0 = (2 * gg + u) * P
-                            words = x_sorted[(t, half)][:, col0 : col0 + P]
-                        else:
-                            words = x_sb[(t, half)][:].bitcast(F32)[:, 256 * gg + u : 256 * (gg + 1) : 2]
-                        nc.tensor.transpose(xt[:, gg, u, :], words, ident[:])
-                grouped = keep.tile([P, 2 * P * 4], BF16, align_bytes=64, name="grouped_%d_%d" % (t, half))
-                nc.scalar.copy(
-                    out=grouped[:].bitcast(F32).rearrange("p (g r u) -> p g r u", g=2, u=2),
-                    in_=xt[:].rearrange("p g u r -> p g r u"),
-                )
-                x_grouped[(t, half)] = grouped
-
-        def quant_x(t):
-            for half in range(2):
-                codes = keep.tile([P, 2 * P], U32, align_bytes=64, name="x_codes_%d_%d" % (t, half))
-                scales = keep.tile([P, 2 * P], U8, align_bytes=64, name="x_scales_%d_%d" % (t, half))
-                nc.vector.quantize_mx(out=codes[:].bitcast(FP8X4), scales=scales[:], in_=x_grouped[(t, half)][:])
-                for gg in range(2):
-                    x_codes[(t, 2 * half + gg)] = codes[:, gg * P : (gg + 1) * P]
-                    x_scales[(t, 2 * half + gg)] = scales[:, gg * P : (gg + 1) * P]
+        def quant_half(t, half):
+            codes = keep.tile([P, 2 * P], U32, align_bytes=64, name="x_codes_%d_%d" % (t, half))
+            scales = keep.tile([P, 2 * P], U8, align_bytes=64, name="x_scales_%d_%d" % (t, half))
+            nc.vector.quantize_mx(out=codes[:].bitcast(FP8X4), scales=scales[:], in_=x_grouped[(t, half)][:])
+            for gg in range(2):
+                x_codes[(t, 2 * half + gg)] = codes[:, gg * P : (gg + 1) * P]
+                x_scales[(t, 2 * half + gg)] = scales[:, gg * P : (gg + 1) * P]
 
         def bank_sums(t, w_tile, w_col0, plane, plane_col0):
             acc = psum.tile([P, BANK], F32, name="acc", tag="bank")
@@ -222,24 +208,29 @@ def tile_rptattention_pa_kernel(
         def zero_plane(plane):
             nc.vector.memset(plane[:].rearrange("p g n -> p (g n)").bitcast(I32), 0)
 
-        turn_x(0)
-        sort_x(1)
-        quant_x(0)
-        turn_x(1)
+        for half in range(2):
+            turn_half(0, half)
+        for half in range(2):
+            quant_half(0, half)
         zero_plane(plane_q_lo)
         load_scale_rows(nc, plane_q_lo, wq_scales, 0, 2 * BANK)
         load_words(nc, w_q_hi, wq_words, 2 * BANK, 2 * BANK)
         load_words(nc, w_v, wv_words, 0, BANK)
-        quant_x(1)
-        sort_x(2)
-        sort_x(3)
+        for half in range(2):
+            turn_half(1, half)
+        for half in range(2):
+            quant_half(1, half)
+        for half in range(2):
+            turn_half(2, half)
+        quant_half(2, 0)
+        turn_half(3, 0, on_vector=True)
+        quant_half(2, 1)
+        turn_half(3, 1, on_vector=True)
+        quant_half(3, 0)
+        quant_half(3, 1)
         make_turns()
         make_factors()
         k_bank(0)
-        turn_x(2)
-        turn_x(3)
-        quant_x(2)
-        quant_x(3)
         k_bank(1)
         k_bank(2)
         k_bank(3)

@@ -30,7 +30,8 @@ ROUND_MAGIC = 12582912.0
 
 FLOPS = 2 * S * D * (2048 + 512 + 512)
 PROD_BUFS = 8
-VECTOR_ADDS = 3
+EARLY_V_BEHIND = [(0, 1), (1024, 0)]
+VECTOR_ADDS = 2
 
 
 def load_scale_rows(nc, plane, scales_dram, col0, width):
@@ -66,8 +67,9 @@ def tile_rptattention_pa_kernel(
 
         plane_k = keep.tile([P, PASSES, BANK], U8, align_bytes=64, name="plane_k")
         plane_q_lo = keep.tile([P, PASSES, 2 * BANK], U8, align_bytes=64, name="plane_q_lo")
+        plane_v = keep.tile([P, PASSES, BANK], U8, align_bytes=64, name="plane_v")
         w_k = keep.tile([P, PASSES, 2 * BANK], U8, align_bytes=64, name="w_k", tag="k_words_then_q_plane")
-        w_q_lo = keep.tile([P, PASSES, 4 * BANK], U8, align_bytes=64, name="w_q_lo", tag="q_words_then_v_plane")
+        w_q_lo = keep.tile([P, PASSES, 4 * BANK], U8, align_bytes=64, name="w_q_lo")
         w_q_hi = keep.tile([P, PASSES, 4 * BANK], U8, align_bytes=64, name="w_q_hi")
         w_v = keep.tile([P, PASSES, 2 * BANK], U8, align_bytes=64, name="w_v")
         pos = keep.tile([P, TOK_TILES], F32, name="pos")
@@ -213,9 +215,11 @@ def tile_rptattention_pa_kernel(
         for half in range(2):
             quant_half(0, half)
         zero_plane(plane_q_lo)
+        zero_plane(plane_v)
         load_scale_rows(nc, plane_q_lo, wq_scales, 0, 2 * BANK)
         load_words(nc, w_q_hi, wq_words, 2 * BANK, 2 * BANK)
         load_words(nc, w_v, wv_words, 0, BANK)
+        load_scale_rows(nc, plane_v, wv_scales, 0, BANK)
         for half in range(2):
             turn_half(1, half)
         for half in range(2):
@@ -236,6 +240,12 @@ def tile_rptattention_pa_kernel(
         k_bank(3)
         plane_q_hi = keep.tile([P, PASSES, 2 * BANK], U8, align_bytes=64, name="plane_q_hi", tag="k_words_then_q_plane")
         load_scale_rows(nc, plane_q_hi, wq_scales, 2 * BANK, 2 * BANK)
+
+        def v_bank(t):
+            acc = bank_sums(t, w_v, 0, plane_v, 0)
+            res = keep.tile([P, BANK], F32, name="res_v_%d" % t)
+            nc.scalar.copy(out=res[:], in_=acc[:])
+            nc.sync.dma_start(out=v_dram[t], in_=res[:])
 
         late_adds = []
         banks_done = 0
@@ -258,15 +268,11 @@ def tile_rptattention_pa_kernel(
                             nc.sync.dma_start(out=out_cols, in_=res_cols)
                 if not at_the_end:
                     nc.sync.dma_start(out=q_dram[t][:, col0 : col0 + 2 * BANK], in_=res[:])
-            if col0 == 0:
-                plane_v = keep.tile([P, PASSES, BANK], U8, align_bytes=64, name="plane_v", tag="q_words_then_v_plane")
-                load_scale_rows(nc, plane_v, wv_scales, 0, BANK)
+                if (col0, t) in EARLY_V_BEHIND:
+                    v_bank(EARLY_V_BEHIND.index((col0, t)))
         for add, out_cols, res_cols in late_adds:
             add()
             nc.sync.dma_start(out=out_cols, in_=res_cols)
 
-        for t in range(TOK_TILES):
-            acc = bank_sums(t, w_v, 0, plane_v, 0)
-            res = keep.tile([P, BANK], F32, name="res_v_%d" % t)
-            nc.scalar.copy(out=res[:], in_=acc[:])
-            nc.sync.dma_start(out=v_dram[t], in_=res[:])
+        for t in range(len(EARLY_V_BEHIND), TOK_TILES):
+            v_bank(t)

@@ -205,7 +205,7 @@ def tile_rptattention_pa_kernel(
             acc = bank_sums(t, w_k, 0, plane_k, 0)
             res = keep.tile([P, BANK], F32, name="res_k_%d" % t)
             rotate(t, acc, res[:], nc.gpsimd)()
-            nc.sync.dma_start(out=k_dram[t], in_=res[:])
+            return res
 
         def zero_plane(plane):
             nc.vector.memset(plane[:].rearrange("p g n -> p (g n)").bitcast(I32), 0)
@@ -217,9 +217,9 @@ def tile_rptattention_pa_kernel(
         zero_plane(plane_q_lo)
         zero_plane(plane_v)
         load_scale_rows(nc, plane_q_lo, wq_scales, 0, 2 * BANK)
-        load_words(nc, w_q_hi, wq_words, 2 * BANK, 2 * BANK)
         load_words(nc, w_v, wv_words, 0, BANK)
         load_scale_rows(nc, plane_v, wv_scales, 0, BANK)
+        load_words(nc, w_q_hi, wq_words, 2 * BANK, 2 * BANK)
         for half in range(2):
             turn_half(1, half)
         for half in range(2):
@@ -234,12 +234,11 @@ def tile_rptattention_pa_kernel(
         quant_half(3, 1)
         make_turns()
         make_factors()
-        k_bank(0)
-        k_bank(1)
-        k_bank(2)
-        k_bank(3)
+        k_res = [k_bank(t) for t in range(TOK_TILES)]
         plane_q_hi = keep.tile([P, PASSES, 2 * BANK], U8, align_bytes=64, name="plane_q_hi", tag="k_words_then_q_plane")
         load_scale_rows(nc, plane_q_hi, wq_scales, 2 * BANK, 2 * BANK)
+        for t in range(TOK_TILES):
+            nc.sync.dma_start(out=k_dram[t], in_=k_res[t][:])
 
         def v_bank(t):
             acc = bank_sums(t, w_v, 0, plane_v, 0)

@@ -78,7 +78,16 @@ def tile_rptattention_pa_kernel(
         )
         ident = keep.tile([P, P], F32, name="ident")
         masks.make_identity(nc, ident[:])
+        idle_in = keep.tile([P, P + BANK], BF16, name="idle_in")
+        nc.vector.memset(idle_in[:], 0.0)
         nc.vector.memset(plane_k[:].rearrange("p g n -> p (g n)").bitcast(I32), 0)
+        idle_out = psum.tile([P, BANK], F32, name="idle_out", tag="bank")
+
+        def idle_matmuls(count):
+            for i in range(count):
+                nc.tensor.matmul(idle_out[:], lhsT=idle_in[:, 0:P], rhs=idle_in[:, P : P + BANK], start=True, stop=True)
+
+        idle_matmuls(4)
 
         x_sb = {}
 
@@ -167,6 +176,8 @@ def tile_rptattention_pa_kernel(
             else:
                 nc.scalar.copy(out=out_words, in_=in_words)
             x_grouped[(t, half)] = grouped
+            if half == 1:
+                idle_matmuls(1)
 
         def quant_half(t, half):
             codes = keep.tile([P, 2 * P], U32, align_bytes=64, name="x_codes_%d_%d" % (t, half))

import math
from contextlib import ExitStack

import concourse.masks as masks
import concourse.mybir as mybir

F32 = mybir.dt.float32
BF16 = mybir.dt.bfloat16
I32 = mybir.dt.int32
U32 = mybir.dt.uint32
U8 = mybir.dt.uint8
FP8X4 = mybir.dt.float8_e4m3fn_x4
FP4X4 = mybir.dt.float4_e2m1fn_x4
ALU = mybir.AluOpType
ACT = mybir.ActivationFunctionType

P = 128
S = 512
D = 2048
HD = 128
PAIRS = HD // 2
K_PASS = 4 * P
PASSES = D // K_PASS
TOK_TILES = S // P
BANK = 512
HEADS_PER_BANK = BANK // HD
ROPE_THETA = 10000.0
FREQ_RATIO = ROPE_THETA ** (-1.0 / PAIRS)
ROUND_MAGIC = 12582912.0

FLOPS = 2 * S * D * (2048 + 512 + 512)
PROD_BUFS = 8
EARLY_V_BEHIND = [(0, 1), (1024, 0)]
VECTOR_ADDS = 2


def load_scale_rows(nc, plane, scales_dram, col0, width):
    rows = scales_dram.bitcast(I32)
    for quad in range(4):
        nc.sync.dma_start(
            out=plane[32 * quad : 32 * quad + 4, :, :].bitcast(I32),
            in_=rows[:, 4 * quad : 4 * quad + 4, col0 // 4 : (col0 + width) // 4].rearrange("g q n -> q g n"),
        )


def load_words(nc, w_tile, words_dram, col0, width):
    nc.sync.dma_start(
        out=w_tile[:].bitcast(I32),
        in_=words_dram.bitcast(I32)[:, :, col0 // 2 : (col0 + width) // 2].rearrange("g p n -> p g n"),
    )


def tile_rptattention_pa_kernel(
    tc, hidden_states, wq_words, wq_scales, wk_words, wk_scales, wv_words, wv_scales, out_0, out_1, out_2
):
    nc = tc.nc
    x_dram = hidden_states[0].rearrange("(t p) k -> t p k", p=P)
    q_dram = out_0[0].rearrange("(t p) h d -> t p (h d)", p=P)
    k_dram = out_1[0].rearrange("(t p) h d -> t p (h d)", p=P)
    v_dram = out_2[0].rearrange("(t p) h d -> t p (h d)", p=P)

    with ExitStack() as ctx:
        keep = ctx.enter_context(tc.tile_pool(name="keep", bufs=1))
        prods = ctx.enter_context(tc.tile_pool(name="prods", bufs=PROD_BUFS))
        psum = ctx.enter_context(tc.psum_pool(name="psum", bufs=8))
        ctx.enter_context(tc.manual_schedule())

        plane_k = keep.tile([P, PASSES, BANK], U8, align_bytes=64, name="plane_k")
        plane_q_lo = keep.tile([P, PASSES, 2 * BANK], U8, align_bytes=64, name="plane_q_lo")
        plane_v = keep.tile([P, PASSES, BANK], U8, align_bytes=64, name="plane_v")
        w_k = keep.tile([P, PASSES, 2 * BANK], U8, align_bytes=64, name="w_k", tag="k_words_then_q_plane")
        w_q_lo = keep.tile([P, PASSES, 4 * BANK], U8, align_bytes=64, name="w_q_lo")
        w_q_hi = keep.tile([P, PASSES, 4 * BANK], U8, align_bytes=64, name="w_q_hi")
        w_v = keep.tile([P, PASSES, 2 * BANK], U8, align_bytes=64, name="w_v")
        pos = keep.tile([P, TOK_TILES], F32, name="pos")
        nc.gpsimd.iota(
            pos[:], pattern=[[P, TOK_TILES]], base=0, channel_multiplier=1, allow_small_or_imprecise_dtypes=True
        )
        ident = keep.tile([P, P], F32, name="ident")
        masks.make_identity(nc, ident[:])
        idle_in = keep.tile([P, P + BANK], BF16, name="idle_in")
        nc.vector.memset(idle_in[:], 0.0)
        nc.vector.memset(plane_k[:].rearrange("p g n -> p (g n)").bitcast(I32), 0)
        idle_out = psum.tile([P, BANK], F32, name="idle_out", tag="bank")

        def idle_matmuls(count):
            for i in range(count):
                nc.tensor.matmul(idle_out[:], lhsT=idle_in[:, 0:P], rhs=idle_in[:, P : P + BANK], start=True, stop=True)

        idle_matmuls(4)

        x_sb = {}

        def load_x(t):
            for half in range(2):
                x_half = keep.tile([P, D // 2], BF16, name="x_%d_%d" % (t, half))
                nc.sync.dma_start(out=x_half[:], in_=x_dram[t][:, half * (D // 2) : (half + 1) * (D // 2)])
                x_sb[(t, half)] = x_half

        load_x(0)
        load_x(1)
        load_x(2)
        load_x(3)
        load_scale_rows(nc, plane_k, wk_scales, 0, BANK)
        load_words(nc, w_k, wk_words, 0, BANK)
        load_words(nc, w_q_lo, wq_words, 0, 2 * BANK)

        ones = keep.tile([P, PAIRS], F32, name="ones")
        nc.vector.memset(ones[:], 1.0)
        nought = keep.tile([P, PAIRS], F32, name="nought")
        nc.vector.memset(nought[:], 0.0)
        warm = keep.tile([P, 1], F32, name="warm")
        nc.scalar.activation(out=warm[:], in_=nought[:, 0:1], func=ACT.Sin)
        ratio = keep.tile([P, PAIRS], F32, name="ratio")
        nc.vector.tensor_scalar(out=ratio[:], in0=ones[:], scalar1=FREQ_RATIO, scalar2=None, op0=ALU.mult)
        freq = keep.tile([P, PAIRS], F32, name="freq")
        nc.vector.tensor_tensor_scan(
            out=freq[:],
            data0=ratio[:],
            data1=nought[:],
            initial=1.0 / (2.0 * math.pi * FREQ_RATIO),
            op0=ALU.mult,
            op1=ALU.add,
        )
        angle = keep.tile([P, TOK_TILES, PAIRS], F32, name="angle")
        nc.vector.tensor_tensor(
            out=angle[:],
            in0=freq[:].unsqueeze(1).to_broadcast([P, TOK_TILES, PAIRS]),
            in1=pos[:].unsqueeze(2).to_broadcast([P, TOK_TILES, PAIRS]),
            op=ALU.mult,
        )
        shifted = keep.tile([P, TOK_TILES, PAIRS], F32, name="shifted")
        nc.vector.tensor_scalar(out=shifted[:], in0=angle[:], scalar1=ROUND_MAGIC, scalar2=None, op0=ALU.add)
        turn = keep.tile([P, TOK_TILES, 3, PAIRS], F32, name="turn")
        nc.vector.scalar_tensor_tensor(
            out=turn[:, :, 0, :],
            in0=shifted[:],
            scalar=ROUND_MAGIC,
            in1=angle[:],
            op0=ALU.subtract,
            op1=ALU.subtract,
        )
        size = keep.tile([P, TOK_TILES, PAIRS], F32, name="size")
        rot_all = keep.tile([P, TOK_TILES, 2, PAIRS, 2], F32, name="rot_all")

        def make_turns():
            nc.scalar.activation(out=size[:], in_=turn[:, :, 0, :], func=ACT.Abs)
            nc.scalar.activation(out=turn[:, :, 1, :], in_=size[:], func=ACT.Copy, scale=-1.0, bias=0.25)
            nc.scalar.activation(out=turn[:, :, 2, :], in_=turn[:, :, 0, :], func=ACT.Copy, scale=-1.0)

        def make_factors():
            for i in range(2):
                nc.scalar.activation(
                    out=rot_all[:, :, i, :, :],
                    in_=turn[:, :, 1 - i : 3 - i, :].rearrange("p t c j -> p t j c"),
                    func=ACT.Sin,
                    scale=2.0 * math.pi,
                )

        x_codes = {}
        x_scales = {}

        x_grouped = {}

        def turn_half(t, half, on_vector=False):
            xt = psum.tile([P, 2, 2, P], F32, name="xt", tag="bank")
            for gg in range(2):
                for u in range(2):
                    words = x_sb[(t, half)][:].bitcast(F32)[:, 256 * gg + u : 256 * (gg + 1) : 2]
                    nc.tensor.transpose(xt[:, gg, u, :], words, ident[:])
            grouped = keep.tile([P, 2 * P * 4], BF16, align_bytes=64, name="grouped_%d_%d" % (t, half))
            out_words = grouped[:].bitcast(F32).rearrange("p (g r u) -> p g r u", g=2, u=2)
            in_words = xt[:].rearrange("p g u r -> p g r u")
            if on_vector:
                nc.vector.tensor_copy(out=out_words, in_=in_words)
            else:
                nc.scalar.copy(out=out_words, in_=in_words)
            x_grouped[(t, half)] = grouped
            if half == 1:
                idle_matmuls(1)

        def quant_half(t, half):
            codes = keep.tile([P, 2 * P], U32, align_bytes=64, name="x_codes_%d_%d" % (t, half))
            scales = keep.tile([P, 2 * P], U8, align_bytes=64, name="x_scales_%d_%d" % (t, half))
            nc.vector.quantize_mx(out=codes[:].bitcast(FP8X4), scales=scales[:], in_=x_grouped[(t, half)][:])
            for gg in range(2):
                x_codes[(t, 2 * half + gg)] = codes[:, gg * P : (gg + 1) * P]
                x_scales[(t, 2 * half + gg)] = scales[:, gg * P : (gg + 1) * P]

        def bank_sums(t, w_tile, w_col0, plane, plane_col0):
            acc = psum.tile([P, BANK], F32, name="acc", tag="bank")
            for g in range(PASSES):
                nc.tensor.matmul_mx(
                    out=acc[:],
                    lhsT=x_codes[(t, g)].bitcast(FP8X4),
                    lhsT_scale=x_scales[(t, g)],
                    rhs=w_tile[:, g, 2 * w_col0 : 2 * (w_col0 + BANK)].bitcast(FP4X4),
                    rhs_scale=plane[:, g, plane_col0 : plane_col0 + BANK],
                    start=(g == 0),
                    stop=(g == PASSES - 1),
                )
            return acc

        def rotate(t, acc, res_cols, add_engine):
            prod = prods.tile([P, 2, BANK], F32, name="prod")
            full = [P, 2, HEADS_PER_BANK, PAIRS, 2]
            nc.vector.tensor_tensor(
                out=prod[:].rearrange("p i (h j o) -> p i h j o", h=HEADS_PER_BANK, o=2),
                in0=acc[:].rearrange("p (h j i) -> p i h j", h=HEADS_PER_BANK, i=2).unsqueeze(4).to_broadcast(full),
                in1=rot_all[:, t].unsqueeze(2).to_broadcast(full),
                op=ALU.mult,
            )
            return lambda: add_engine.tensor_tensor(out=res_cols, in0=prod[:, 0, :], in1=prod[:, 1, :], op=ALU.add)

        def k_bank(t):
            acc = bank_sums(t, w_k, 0, plane_k, 0)
            res = keep.tile([P, BANK], F32, name="res_k_%d" % t)
            rotate(t, acc, res[:], nc.gpsimd)()
            return res

        def zero_plane(plane):
            nc.vector.memset(plane[:].rearrange("p g n -> p (g n)").bitcast(I32), 0)

        for half in range(2):
            turn_half(0, half)
        for half in range(2):
            quant_half(0, half)
        zero_plane(plane_q_lo)
        zero_plane(plane_v)
        load_scale_rows(nc, plane_q_lo, wq_scales, 0, 2 * BANK)
        load_words(nc, w_v, wv_words, 0, BANK)
        load_scale_rows(nc, plane_v, wv_scales, 0, BANK)
        load_words(nc, w_q_hi, wq_words, 2 * BANK, 2 * BANK)
        for half in range(2):
            turn_half(1, half)
        for half in range(2):
            quant_half(1, half)
        for half in range(2):
            turn_half(2, half)
        quant_half(2, 0)
        turn_half(3, 0, on_vector=True)
        quant_half(2, 1)
        turn_half(3, 1, on_vector=True)
        quant_half(3, 0)
        quant_half(3, 1)
        make_turns()
        make_factors()
        k_res = [k_bank(t) for t in range(TOK_TILES)]
        plane_q_hi = keep.tile([P, PASSES, 2 * BANK], U8, align_bytes=64, name="plane_q_hi", tag="k_words_then_q_plane")
        load_scale_rows(nc, plane_q_hi, wq_scales, 2 * BANK, 2 * BANK)
        for t in range(TOK_TILES):
            nc.sync.dma_start(out=k_dram[t], in_=k_res[t][:])

        def v_bank(t):
            acc = bank_sums(t, w_v, 0, plane_v, 0)
            res = keep.tile([P, BANK], F32, name="res_v_%d" % t)
            nc.scalar.copy(out=res[:], in_=acc[:])
            nc.sync.dma_start(out=v_dram[t], in_=res[:])

        late_adds = []
        banks_done = 0
        for w_tile, plane, col0 in ((w_q_lo, plane_q_lo, 0), (w_q_hi, plane_q_hi, 2 * BANK)):
            for t in range(TOK_TILES):
                at_the_end = col0 > 0 and t >= TOK_TILES - 2
                res = keep.tile([P, 2 * BANK], F32, name="res_q_%d_%d" % (t, col0))
                for b in range(2):
                    acc = bank_sums(t, w_tile, BANK * b, plane, BANK * b)
                    res_cols = res[:, BANK * b : BANK * (b + 1)]
                    out_cols = q_dram[t][:, col0 + BANK * b : col0 + BANK * (b + 1)]
                    on_vector = banks_done >= 4 * TOK_TILES - VECTOR_ADDS
                    banks_done += 1
                    add = rotate(t, acc, res_cols, nc.vector if on_vector else nc.gpsimd)
                    if on_vector:
                        late_adds.append((add, out_cols, res_cols))
                    else:
                        add()
                        if at_the_end:
                            nc.sync.dma_start(out=out_cols, in_=res_cols)
                if not at_the_end:
                    nc.sync.dma_start(out=q_dram[t][:, col0 : col0 + 2 * BANK], in_=res[:])
                if (col0, t) in EARLY_V_BEHIND:
                    v_bank(EARLY_V_BEHIND.index((col0, t)))
        for add, out_cols, res_cols in late_adds:
            add()
            nc.sync.dma_start(out=out_cols, in_=res_cols)

        for t in range(len(EARLY_V_BEHIND), TOK_TILES):
            v_bank(t)
